import numpy as np
import ml_dtypes


def mxq(x, axis, fmt="e4m3"):
    dtype, down = {"e4m3": (ml_dtypes.float8_e4m3fn, 7), "e5m2": (ml_dtypes.float8_e5m2, 14)}[fmt]
    v = np.moveaxis(np.asarray(x, np.float32).astype(ml_dtypes.bfloat16).astype(np.float64), axis, -1)
    blocks = v.reshape(v.shape[:-1] + (-1, 32))
    amax = np.abs(blocks).max(-1, keepdims=True)
    byte = np.maximum(np.where(amax > 0, np.frexp(amax)[1] - 1 + 127, 0) - down, 1)
    scale = np.exp2(byte - 127.0)
    codes = (blocks / scale).astype(np.float32).astype(dtype).astype(np.float64)
    return np.moveaxis((codes * scale).reshape(v.shape), -1, axis)


WIDE = False


def mx_kscale(k):
    if not WIDE:
        return np.ones(k)
    levels = np.array([10, -10, 5, -5, 0])
    a = np.random.permutation(np.resize(levels, k // 512 * 4)).reshape(k // 512, 4)
    idx = np.arange(k)
    return np.exp2(a[idx // 512, idx % 128 // 32])


BF16 = ml_dtypes.bfloat16


def bf(x):
    return np.asarray(x, np.float32).astype(BF16)


def f64(x):
    return np.asarray(x).astype(np.float64)


B, L, C, H, F = 2, 512, 512, 4, 2048
FH = F // 2
EPS = 1e-5


def layer_norm(x, g, b):
    mu = x.mean(-1, keepdims=True)
    var = np.square(x - mu).mean(-1, keepdims=True)
    return (x - mu) / np.sqrt(var + EPS) * g + b


def setup_inputs():
    s = mx_kscale(C)
    return {"x_attn": bf(np.random.standard_normal((B, L, C))),
            "adj": bf(np.random.randint(0, 2, (B, L, L))),
            "ln2_g": bf((1.0 + 0.1 * np.random.standard_normal(C)) * s),
            "ln2_b": bf(0.1 * np.random.standard_normal(C) * s),
            "w_fc1": bf(np.random.standard_normal((C, F)) / np.sqrt(C) / s[:, None]),
            "w_gcn": bf(np.random.standard_normal((C, F)) * 2.0 / np.sqrt(L) / np.sqrt(C) / s[:, None])}


def reference(x_attn, adj, ln2_g, ln2_b, w_fc1, w_gcn):
    ad = f64(adj)
    xn = mxq(layer_norm(f64(x_attn), f64(ln2_g), f64(ln2_b)), 2, "e4m3")
    h = xn @ mxq(f64(w_fc1), 0, "e4m3")
    g = mxq(xn @ mxq(f64(w_gcn), 0, "e4m3"), 1, "e4m3")
    fwd = mxq(ad, 2, "e4m3") @ g[..., :FH]
    bwd = mxq(ad, 1, "e4m3").transpose(0, 2, 1) @ g[..., FH:]
    return np.maximum(h + np.concatenate([fwd, bwd], axis=-1), 0.0)

@@ -1,0 +1,225 @@
+from contextlib import ExitStack
+
+import concourse.masks as masks
+import concourse.mybir as mybir
+
+F32 = mybir.dt.float32
+BF16 = mybir.dt.bfloat16
+U32 = mybir.dt.uint32
+U8 = mybir.dt.uint8
+FP8X4 = mybir.dt.float8_e4m3fn_x4
+ACT = mybir.ActivationFunctionType
+ALU = mybir.AluOpType
+
+P = 128
+PACK = 4
+GRAPHS = 2
+NODES = 512
+FEATS = 512
+HIDDEN = 2048
+HALF = HIDDEN // 2
+BLOCK = 512
+N_BLOCKS = HIDDEN // BLOCK
+EPS = 1e-5
+RUN = 4
+SCALAR_BLOCKS = 2
+
+FLOPS = 2 * GRAPHS * NODES * FEATS * 2 * HIDDEN + 2 * GRAPHS * NODES * NODES * HIDDEN
+
+
+def interleave_rows(copy, grouped, rows):
+    copy(
+        out=grouped.rearrange("p (c i) t -> p c t i", i=RUN),
+        in_=rows.rearrange("p t (c i) -> p c t i", i=RUN),
+    )
+
+
+def quantise(nc, codes, scales, grouped):
+    nc.vector.quantize_mx(
+        out=codes.bitcast(FP8X4),
+        scales=scales,
+        in_=grouped.rearrange("p n t -> p (n t)"),
+    )
+
+
+def tile_encoderblock_pb_kernel(tc, x_attn, adj, ln2_g, ln2_b, w_fc1, w_gcn, out):
+    nc = tc.nc
+    with ExitStack() as ctx:
+        keep = ctx.enter_context(tc.tile_pool(name="keep", bufs=1))
+        stage = ctx.enter_context(tc.tile_pool(name="stage", bufs=3))
+        results = ctx.enter_context(tc.tile_pool(name="results", bufs=8))
+        psum = ctx.enter_context(tc.psum_pool(name="psum", bufs=8))
+
+        x_sb = [keep.tile([P, PACK, FEATS], BF16, name="x_sb%d" % b) for b in range(GRAPHS)]
+        adj_sb = [keep.tile([P, PACK, NODES], BF16, name="adj_sb%d" % b) for b in range(GRAPHS)]
+        wg_raw = keep.tile([P, PACK, HIDDEN], BF16, name="wg_raw")
+        wf_raw = keep.tile([P, PACK, HIDDEN], BF16, name="wf_raw")
+
+        def mx_operand(name, width):
+            codes = keep.tile([P, width], U32, name=name + "_codes", align_bytes=64)
+            scales = keep.tile([P, width], U8, name=name + "_scales", align_bytes=64)
+            return codes, scales
+
+        xn_q = [mx_operand("xn%d" % b, NODES) for b in range(GRAPHS)]
+        fwd_q = [mx_operand("fwd%d" % b, NODES) for b in range(GRAPHS)]
+        bwd_q = [mx_operand("bwd%d" % b, NODES) for b in range(GRAPHS)]
+        g_q = [mx_operand("g%d" % b, HIDDEN) for b in range(GRAPHS)]
+        wg_q = mx_operand("wg", HIDDEN)
+        wf_q = mx_operand("wf", HIDDEN)
+
+        params_bf = keep.tile([P, P], BF16, name="params_bf")
+        nc.vector.memset(params_bf[:], 0.0)
+        nc.scalar.dma_start(out=params_bf[0:PACK, :], in_=ln2_g.rearrange("(u c) -> u c", c=P))
+        nc.scalar.dma_start(out=params_bf[PACK : 2 * PACK, :], in_=ln2_b.rearrange("(u c) -> u c", c=P))
+
+        def load_nodes(dst, src):
+            nc.sync.dma_start(out=dst[:], in_=src.rearrange("(p t) c -> p t c", t=PACK))
+
+        def load_weight_block(dst, src, blk):
+            cols = slice(blk * BLOCK, (blk + 1) * BLOCK)
+            nc.sync.dma_start(out=dst[:, :, cols], in_=src.rearrange("(u p) n -> p u n", p=P)[:, :, cols])
+
+        load_nodes(x_sb[0], x_attn[0])
+        load_weight_block(wg_raw, w_gcn, 0)
+        load_nodes(x_sb[1], x_attn[1])
+        load_weight_block(wf_raw, w_fc1, 0)
+        load_nodes(adj_sb[0], adj[0])
+        load_nodes(adj_sb[1], adj[1])
+        for blk in range(1, N_BLOCKS):
+            load_weight_block(wg_raw, w_gcn, blk)
+            load_weight_block(wf_raw, w_fc1, blk)
+
+        ident = keep.tile([P, P], F32, name="ident")
+        masks.make_identity(nc, ident[:])
+        eps_col = keep.tile([P, 1], F32, name="eps_col")
+        nc.vector.memset(eps_col[:], EPS)
+
+        params_f32 = keep.tile([P, P], F32, name="params_f32")
+        nc.vector.tensor_copy(out=params_f32[:], in_=params_bf[:])
+        params_t = psum.tile([P, P], F32, tag="bank", name="params_t")
+        nc.tensor.transpose(params_t[:], params_f32[:], ident[:])
+        ln_cols = keep.tile([P, 2 * PACK], F32, name="ln_cols")
+        nc.vector.tensor_copy(out=ln_cols[:], in_=params_t[:, 0 : 2 * PACK])
+
+        def layer_norm(b):
+            stats = stage.tile([P, PACK, 6], F32, name="stats")
+            mean_var = stage.tile([P, PACK, 2], F32, name="mean_var")
+            for t in range(PACK):
+                nc.vector.bn_stats(out=stats[:, t, :], in_=x_sb[b][:, t, :])
+            for t in range(PACK):
+                nc.vector.bn_aggr(out=mean_var[:, t, :], in_=stats[:, t, :])
+            std = stage.tile([P, PACK], F32, name="std")
+            nc.scalar.activation(out=std[:], in_=mean_var[:, :, 1], func=ACT.Sqrt, bias=eps_col[:])
+            rstd = stage.tile([P, PACK], F32, name="rstd")
+            nc.vector.reciprocal(out=rstd[:], in_=std[:])
+            xhat = stage.tile([P, PACK, FEATS], F32, name="xhat", bufs=2)
+            for t in range(PACK):
+                nc.vector.tensor_scalar(
+                    out=xhat[:, t, :],
+                    in0=x_sb[b][:, t, :],
+                    scalar1=mean_var[:, t, 0:1],
+                    scalar2=rstd[:, t : t + 1],
+                    op0=ALU.subtract,
+                    op1=ALU.mult,
+                )
+            planes = stage.tile([P, PACK, NODES], BF16, name="planes", bufs=2)
+            for u in range(PACK):
+                bank = psum.tile([P, PACK, P], F32, tag="bank", name="xt_bank")
+                for t in range(PACK):
+                    nc.tensor.transpose(bank[:, t, :], xhat[:, t, u * P : (u + 1) * P], ident[:])
+                flat = bank[:].rearrange("p t n -> p (t n)")
+                gain = ln_cols[:, u : u + 1]
+                bias = ln_cols[:, PACK + u : PACK + u + 1]
+                if u % 2 == 0:
+                    nc.scalar.activation(out=planes[:, u, :], in_=flat, func=ACT.Identity, scale=gain, bias=bias)
+                else:
+                    nc.vector.tensor_scalar(
+                        out=planes[:, u, :], in0=flat, scalar1=gain, scalar2=bias, op0=ALU.mult, op1=ALU.add
+                    )
+            grouped = stage.tile([P, NODES, PACK], BF16, name="xn_grouped", bufs=2, align_bytes=64)
+            interleave_rows(nc.vector.tensor_copy, grouped[:], planes[:])
+            quantise(nc, xn_q[b][0][:], xn_q[b][1][:], grouped[:])
+
+        def prepare_weight_block(raw, w_q, blk):
+            cols = slice(blk * BLOCK, (blk + 1) * BLOCK)
+            grouped = stage.tile([P, BLOCK, PACK], BF16, name="w_grouped", align_bytes=64)
+            copy = nc.scalar.copy if blk < SCALAR_BLOCKS else nc.vector.tensor_copy
+            interleave_rows(copy, grouped[:], raw[:, :, cols])
+            quantise(nc, w_q[0][:, cols], w_q[1][:, cols], grouped[:])
+
+        def prepare_backward(b):
+            grouped = stage.tile([P, NODES, PACK], BF16, name="bwd_grouped", bufs=2, align_bytes=64)
+            nc.vector.tensor_copy(
+                out=grouped[:].rearrange("p (s m) t -> p m t s", s=PACK),
+                in_=adj_sb[b][:].rearrange("p t (m s) -> p m t s", s=PACK),
+            )
+            quantise(nc, bwd_q[b][0][:], bwd_q[b][1][:], grouped[:])
+
+        def prepare_forward(b):
+            words = adj_sb[b][:].rearrange("p s j -> p (s j)").bitcast(F32)
+            words = words.rearrange("p (s q v) -> p s v q", s=PACK, v=2)
+            grouped = stage.tile([P, NODES * PACK], BF16, name="fwd_grouped", bufs=2, align_bytes=64)
+            grouped_words = grouped[:].bitcast(F32).rearrange("p (s m v) -> p s m v", s=PACK, v=2)
+            for pair in range(PACK // 2):
+                bank = psum.tile([P, 2, 2, P], F32, tag="bank", name="adjt_bank")
+                for s2 in range(2):
+                    for v in range(2):
+                        nc.tensor.transpose(bank[:, s2, v, :], words[:, 2 * pair + s2, v, :], ident[:])
+                nc.scalar.copy(
+                    out=grouped_words[:, 2 * pair : 2 * pair + 2, :, :],
+                    in_=bank[:].rearrange("p s v m -> p s m v"),
+                )
+            quantise(nc, fwd_q[b][0][:], fwd_q[b][1][:], grouped[:].rearrange("p (n t) -> p n t", t=PACK))
+
+        def mx_pass(acc, stationary, s, moving, cols, start, stop):
+            rows = slice(s * P, (s + 1) * P)
+            nc.tensor.matmul_mx(
+                out=acc,
+                lhsT=stationary[0][:, rows].bitcast(FP8X4),
+                lhsT_scale=stationary[1][:, rows],
+                rhs=moving[0][:, cols].bitcast(FP8X4),
+                rhs_scale=moving[1][:, cols],
+                start=start,
+                stop=stop,
+            )
+
+        def g_unit(b, blk):
+            grouped = stage.tile([P, BLOCK, PACK], BF16, name="g_grouped", align_bytes=64)
+            for q in range(BLOCK // P):
+                bank = psum.tile([P, PACK, P], F32, tag="bank", name="g_bank")
+                cols = slice(blk * BLOCK + q * P, blk * BLOCK + (q + 1) * P)
+                for t in range(PACK):
+                    mx_pass(bank[:, t, :], xn_q[b], t, wg_q, cols, True, True)
+                nc.scalar.copy(out=grouped[:, q * P : (q + 1) * P, :], in_=bank[:].rearrange("p t w -> p w t"))
+            cols = slice(blk * BLOCK, (blk + 1) * BLOCK)
+            quantise(nc, g_q[b][0][:, cols], g_q[b][1][:, cols], grouped[:])
+
+        def out_unit(b, blk):
+            cols = slice(blk * BLOCK, (blk + 1) * BLOCK)
+            adj_q = fwd_q[b] if blk * BLOCK < HALF else bwd_q[b]
+            out_rows = out[b].rearrange("(m s) f -> m s f", s=PACK)
+            for s in range(PACK):
+                acc = psum.tile([P, BLOCK], F32, tag="bank", name="acc")
+                mx_pass(acc[:], xn_q[b], s, wf_q, cols, True, False)
+                mx_pass(acc[:], adj_q, s, g_q[b], cols, False, True)
+                res = results.tile([P, BLOCK], F32, name="res")
+                if s % 2 == 1:
+                    nc.vector.tensor_scalar_max(out=res[:], in0=acc[:], scalar1=0.0)
+                else:
+                    nc.scalar.activation(out=res[:], in_=acc[:], func=ACT.Relu)
+                nc.sync.dma_start(out=out_rows[:, s, cols], in_=res[:])
+
+        for blk in range(N_BLOCKS):
+            for b in range(GRAPHS):
+                if blk == 0:
+                    layer_norm(b)
+                if b == 0:
+                    prepare_weight_block(wg_raw, wg_q, blk)
+                g_unit(b, blk)
+                if blk == 0:
+                    prepare_forward(b)
+                if blk * BLOCK == HALF:
+                    prepare_backward(b)
+                if b == 0:
+                    prepare_weight_block(wf_raw, wf_q, blk)
+                out_unit(b, blk)

@@ -20,31 +20,32 @@ HIDDEN = 2048
 HALF = HIDDEN // 2
 BLOCK = 512
 N_BLOCKS = HIDDEN // BLOCK
+AHEAD = 2
 EPS = 1e-5
-RUN = 4
-SCALAR_BLOCKS = 2
 
 FLOPS = 2 * GRAPHS * NODES * FEATS * 2 * HIDDEN + 2 * GRAPHS * NODES * NODES * HIDDEN
 
-
-def interleave_rows(copy, grouped, rows):
-    copy(
-        out=grouped.rearrange("p (c i) t -> p c t i", i=RUN),
-        in_=rows.rearrange("p t (c i) -> p c t i", i=RUN),
-    )
+IN_ORDER = "p (c i) t -> p c t i"
+BY_RESIDUE = "p (i c) t -> p c t i"
 
 
-def quantise(nc, codes, scales, grouped):
-    nc.vector.quantize_mx(
-        out=codes.bitcast(FP8X4),
-        scales=scales,
-        in_=grouped.rearrange("p n t -> p (n t)"),
-    )
+def block_cols(blk):
+    return slice(blk * BLOCK, (blk + 1) * BLOCK)
+
+
+def interleave_rows(copy, grouped, order, rows):
+    copy(out=grouped.rearrange(order, i=PACK), in_=rows.rearrange("p t (c i) -> p c t i", i=PACK))
+
+
+def quantise(nc, operand, grouped):
+    codes, scales = operand
+    nc.vector.quantize_mx(out=codes.bitcast(FP8X4), scales=scales, in_=grouped.rearrange("p n t -> p (n t)"))
 
 
 def tile_encoderblock_pb_kernel(tc, x_attn, adj, ln2_g, ln2_b, w_fc1, w_gcn, out):
     nc = tc.nc
     with ExitStack() as ctx:
+        ctx.enter_context(tc.manual_schedule())
         keep = ctx.enter_context(tc.tile_pool(name="keep", bufs=1))
         stage = ctx.enter_context(tc.tile_pool(name="stage", bufs=3))
         results = ctx.enter_context(tc.tile_pool(name="results", bufs=8))
@@ -52,13 +53,16 @@ def tile_encoderblock_pb_kernel(tc, x_attn, adj, ln2_g, ln2_b, w_fc1, w_gcn, out
 
         x_sb = [keep.tile([P, PACK, FEATS], BF16, name="x_sb%d" % b) for b in range(GRAPHS)]
         adj_sb = [keep.tile([P, PACK, NODES], BF16, name="adj_sb%d" % b) for b in range(GRAPHS)]
-        wg_raw = keep.tile([P, PACK, HIDDEN], BF16, name="wg_raw")
-        wf_raw = keep.tile([P, PACK, HIDDEN], BF16, name="wf_raw")
+        wg_raw = [keep.tile([P, PACK, BLOCK], BF16, name="wg_raw%d" % blk) for blk in range(N_BLOCKS)]
+        wf_raw = [keep.tile([P, PACK, BLOCK], BF16, name="wf_raw%d" % blk) for blk in range(N_BLOCKS)]
 
         def mx_operand(name, width):
             codes = keep.tile([P, width], U32, name=name + "_codes", align_bytes=64)
             scales = keep.tile([P, width], U8, name=name + "_scales", align_bytes=64)
             return codes, scales
+
+        def columns(operand, cols):
+            return operand[0][:, cols], operand[1][:, cols]
 
         xn_q = [mx_operand("xn%d" % b, NODES) for b in range(GRAPHS)]
         fwd_q = [mx_operand("fwd%d" % b, NODES) for b in range(GRAPHS)]
@@ -67,99 +71,83 @@ def tile_encoderblock_pb_kernel(tc, x_attn, adj, ln2_g, ln2_b, w_fc1, w_gcn, out
         wg_q = mx_operand("wg", HIDDEN)
         wf_q = mx_operand("wf", HIDDEN)
 
-        params_bf = keep.tile([P, P], BF16, name="params_bf")
-        nc.vector.memset(params_bf[:], 0.0)
-        nc.scalar.dma_start(out=params_bf[0:PACK, :], in_=ln2_g.rearrange("(u c) -> u c", c=P))
-        nc.scalar.dma_start(out=params_bf[PACK : 2 * PACK, :], in_=ln2_b.rearrange("(u c) -> u c", c=P))
+        params_rows = keep.tile([2 * PACK, P], BF16, name="params_rows")
+        nc.scalar.dma_start(out=params_rows[0:PACK, :], in_=ln2_g.rearrange("(u c) -> u c", c=P))
+        nc.scalar.dma_start(out=params_rows[PACK : 2 * PACK, :], in_=ln2_b.rearrange("(u c) -> u c", c=P))
 
         def load_nodes(dst, src):
             nc.sync.dma_start(out=dst[:], in_=src.rearrange("(p t) c -> p t c", t=PACK))
 
         def load_weight_block(dst, src, blk):
-            cols = slice(blk * BLOCK, (blk + 1) * BLOCK)
-            nc.sync.dma_start(out=dst[:, :, cols], in_=src.rearrange("(u p) n -> p u n", p=P)[:, :, cols])
+            nc.sync.dma_start(out=dst[blk][:], in_=src.rearrange("(u p) n -> p u n", p=P)[:, :, block_cols(blk)])
 
         load_nodes(x_sb[0], x_attn[0])
         load_weight_block(wg_raw, w_gcn, 0)
         load_nodes(x_sb[1], x_attn[1])
         load_weight_block(wf_raw, w_fc1, 0)
+        load_weight_block(wg_raw, w_gcn, 1)
+        load_weight_block(wf_raw, w_fc1, 1)
         load_nodes(adj_sb[0], adj[0])
         load_nodes(adj_sb[1], adj[1])
-        for blk in range(1, N_BLOCKS):
+        for blk in range(AHEAD, N_BLOCKS):
             load_weight_block(wg_raw, w_gcn, blk)
             load_weight_block(wf_raw, w_fc1, blk)
 
-        ident = keep.tile([P, P], F32, name="ident")
-        masks.make_identity(nc, ident[:])
-        eps_col = keep.tile([P, 1], F32, name="eps_col")
-        nc.vector.memset(eps_col[:], EPS)
+        def interleave_weight_block(copy, raw, blk):
+            grouped = stage.tile([P, BLOCK, PACK], BF16, name="w_grouped", bufs=4, align_bytes=64)
+            interleave_rows(copy, grouped[:], IN_ORDER, raw[blk][:])
+            return grouped
 
-        params_f32 = keep.tile([P, P], F32, name="params_f32")
-        nc.vector.tensor_copy(out=params_f32[:], in_=params_bf[:])
-        params_t = psum.tile([P, P], F32, tag="bank", name="params_t")
-        nc.tensor.transpose(params_t[:], params_f32[:], ident[:])
-        ln_cols = keep.tile([P, 2 * PACK], F32, name="ln_cols")
-        nc.vector.tensor_copy(out=ln_cols[:], in_=params_t[:, 0 : 2 * PACK])
+        stats = keep.tile([P, GRAPHS * PACK, 6], F32, name="stats")
+        mean_var = keep.tile([P, GRAPHS * PACK, 2], F32, name="mean_var")
+        std = keep.tile([P, GRAPHS * PACK], F32, name="std")
+        rstd = keep.tile([P, GRAPHS * PACK], F32, name="rstd")
+        xhat = [keep.tile([P, PACK, FEATS], F32, name="xhat%d" % b) for b in range(GRAPHS)]
+        planes = [keep.tile([P, PACK, NODES], BF16, name="planes%d" % b) for b in range(GRAPHS)]
 
-        def layer_norm(b):
-            stats = stage.tile([P, PACK, 6], F32, name="stats")
-            mean_var = stage.tile([P, PACK, 2], F32, name="mean_var")
+        def statistics(b):
             for t in range(PACK):
-                nc.vector.bn_stats(out=stats[:, t, :], in_=x_sb[b][:, t, :])
+                nc.vector.bn_stats(out=stats[:, b * PACK + t, :], in_=x_sb[b][:, t, :])
             for t in range(PACK):
-                nc.vector.bn_aggr(out=mean_var[:, t, :], in_=stats[:, t, :])
-            std = stage.tile([P, PACK], F32, name="std")
-            nc.scalar.activation(out=std[:], in_=mean_var[:, :, 1], func=ACT.Sqrt, bias=eps_col[:])
-            rstd = stage.tile([P, PACK], F32, name="rstd")
-            nc.vector.reciprocal(out=rstd[:], in_=std[:])
-            xhat = stage.tile([P, PACK, FEATS], F32, name="xhat", bufs=2)
+                nc.vector.bn_aggr(out=mean_var[:, b * PACK + t, :], in_=stats[:, b * PACK + t, :])
+
+        def normalise(b):
             for t in range(PACK):
                 nc.vector.tensor_scalar(
-                    out=xhat[:, t, :],
+                    out=xhat[b][:, t, :],
                     in0=x_sb[b][:, t, :],
-                    scalar1=mean_var[:, t, 0:1],
-                    scalar2=rstd[:, t : t + 1],
+                    scalar1=mean_var[:, b * PACK + t, 0:1],
+                    scalar2=rstd[:, b * PACK + t : b * PACK + t + 1],
                     op0=ALU.subtract,
                     op1=ALU.mult,
                 )
-            planes = stage.tile([P, PACK, NODES], BF16, name="planes", bufs=2)
+
+        def transpose_xn(b):
             for u in range(PACK):
                 bank = psum.tile([P, PACK, P], F32, tag="bank", name="xt_bank")
                 for t in range(PACK):
-                    nc.tensor.transpose(bank[:, t, :], xhat[:, t, u * P : (u + 1) * P], ident[:])
+                    nc.tensor.transpose(bank[:, t, :], xhat[b][:, t, u * P : (u + 1) * P], ident[:])
                 flat = bank[:].rearrange("p t n -> p (t n)")
                 gain = ln_cols[:, u : u + 1]
-                bias = ln_cols[:, PACK + u : PACK + u + 1]
+                shift = ln_cols[:, PACK + u : PACK + u + 1]
                 if u % 2 == 0:
-                    nc.scalar.activation(out=planes[:, u, :], in_=flat, func=ACT.Identity, scale=gain, bias=bias)
+                    nc.scalar.activation(out=planes[b][:, u, :], in_=flat, func=ACT.Identity, scale=gain, bias=shift)
                 else:
                     nc.vector.tensor_scalar(
-                        out=planes[:, u, :], in0=flat, scalar1=gain, scalar2=bias, op0=ALU.mult, op1=ALU.add
+                        out=planes[b][:, u, :], in0=flat, scalar1=gain, scalar2=shift, op0=ALU.mult, op1=ALU.add
                     )
+
+        def interleave_xn(b):
             grouped = stage.tile([P, NODES, PACK], BF16, name="xn_grouped", bufs=2, align_bytes=64)
-            interleave_rows(nc.vector.tensor_copy, grouped[:], planes[:])
-            quantise(nc, xn_q[b][0][:], xn_q[b][1][:], grouped[:])
+            interleave_rows(nc.vector.tensor_copy, grouped[:], IN_ORDER, planes[b][:])
+            return grouped
 
-        def prepare_weight_block(raw, w_q, blk):
-            cols = slice(blk * BLOCK, (blk + 1) * BLOCK)
-            grouped = stage.tile([P, BLOCK, PACK], BF16, name="w_grouped", align_bytes=64)
-            copy = nc.scalar.copy if blk < SCALAR_BLOCKS else nc.vector.tensor_copy
-            interleave_rows(copy, grouped[:], raw[:, :, cols])
-            quantise(nc, w_q[0][:, cols], w_q[1][:, cols], grouped[:])
-
-        def prepare_backward(b):
-            grouped = stage.tile([P, NODES, PACK], BF16, name="bwd_grouped", bufs=2, align_bytes=64)
-            nc.vector.tensor_copy(
-                out=grouped[:].rearrange("p (s m) t -> p m t s", s=PACK),
-                in_=adj_sb[b][:].rearrange("p t (m s) -> p m t s", s=PACK),
-            )
-            quantise(nc, bwd_q[b][0][:], bwd_q[b][1][:], grouped[:])
-
-        def prepare_forward(b):
+        def transpose_adjacency(b):
             words = adj_sb[b][:].rearrange("p s j -> p (s j)").bitcast(F32)
             words = words.rearrange("p (s q v) -> p s v q", s=PACK, v=2)
-            grouped = stage.tile([P, NODES * PACK], BF16, name="fwd_grouped", bufs=2, align_bytes=64)
-            grouped_words = grouped[:].bitcast(F32).rearrange("p (s m v) -> p s m v", s=PACK, v=2)
+            grouped = stage.tile([P, NODES, PACK], BF16, name="fwd_grouped", bufs=2, align_bytes=64)
+            grouped_words = grouped[:].rearrange("p n t -> p (n t)").bitcast(F32)
+            grouped_words = grouped_words.rearrange("p (s m v) -> p s m v", s=PACK, v=2)
             for pair in range(PACK // 2):
                 bank = psum.tile([P, 2, 2, P], F32, tag="bank", name="adjt_bank")
                 for s2 in range(2):
@@ -169,21 +157,22 @@ def tile_encoderblock_pb_kernel(tc, x_attn, adj, ln2_g, ln2_b, w_fc1, w_gcn, out
                     out=grouped_words[:, 2 * pair : 2 * pair + 2, :, :],
                     in_=bank[:].rearrange("p s v m -> p s m v"),
                 )
-            quantise(nc, fwd_q[b][0][:], fwd_q[b][1][:], grouped[:].rearrange("p (n t) -> p n t", t=PACK))
+            return grouped
 
         def mx_pass(acc, stationary, s, moving, cols, start, stop):
-            rows = slice(s * P, (s + 1) * P)
+            lhs_codes, lhs_scales = columns(stationary, slice(s * P, (s + 1) * P))
+            rhs_codes, rhs_scales = columns(moving, cols)
             nc.tensor.matmul_mx(
                 out=acc,
-                lhsT=stationary[0][:, rows].bitcast(FP8X4),
-                lhsT_scale=stationary[1][:, rows],
-                rhs=moving[0][:, cols].bitcast(FP8X4),
-                rhs_scale=moving[1][:, cols],
+                lhsT=lhs_codes.bitcast(FP8X4),
+                lhsT_scale=lhs_scales,
+                rhs=rhs_codes.bitcast(FP8X4),
+                rhs_scale=rhs_scales,
                 start=start,
                 stop=stop,
             )
 
-        def g_unit(b, blk):
+        def g_matmuls(b, blk):
             grouped = stage.tile([P, BLOCK, PACK], BF16, name="g_grouped", align_bytes=64)
             for q in range(BLOCK // P):
                 bank = psum.tile([P, PACK, P], F32, tag="bank", name="g_bank")
@@ -191,11 +180,10 @@ def tile_encoderblock_pb_kernel(tc, x_attn, adj, ln2_g, ln2_b, w_fc1, w_gcn, out
                 for t in range(PACK):
                     mx_pass(bank[:, t, :], xn_q[b], t, wg_q, cols, True, True)
                 nc.scalar.copy(out=grouped[:, q * P : (q + 1) * P, :], in_=bank[:].rearrange("p t w -> p w t"))
-            cols = slice(blk * BLOCK, (blk + 1) * BLOCK)
-            quantise(nc, g_q[b][0][:, cols], g_q[b][1][:, cols], grouped[:])
+            return grouped
 
-        def out_unit(b, blk):
-            cols = slice(blk * BLOCK, (blk + 1) * BLOCK)
+        def out_matmuls(b, blk):
+            cols = block_cols(blk)
             adj_q = fwd_q[b] if blk * BLOCK < HALF else bwd_q[b]
             out_rows = out[b].rearrange("(m s) f -> m s f", s=PACK)
             for s in range(PACK):
@@ -203,23 +191,69 @@ def tile_encoderblock_pb_kernel(tc, x_attn, adj, ln2_g, ln2_b, w_fc1, w_gcn, out
                 mx_pass(acc[:], xn_q[b], s, wf_q, cols, True, False)
                 mx_pass(acc[:], adj_q, s, g_q[b], cols, False, True)
                 res = results.tile([P, BLOCK], F32, name="res")
-                if s % 2 == 1:
-                    nc.vector.tensor_scalar_max(out=res[:], in0=acc[:], scalar1=0.0)
-                else:
+                if s % 2 == 0:
                     nc.scalar.activation(out=res[:], in_=acc[:], func=ACT.Relu)
+                else:
+                    nc.vector.tensor_scalar_max(out=res[:], in0=acc[:], scalar1=0.0)
                 nc.sync.dma_start(out=out_rows[:, s, cols], in_=res[:])
 
-        for blk in range(N_BLOCKS):
-            for b in range(GRAPHS):
-                if blk == 0:
-                    layer_norm(b)
-                if b == 0:
-                    prepare_weight_block(wg_raw, wg_q, blk)
-                g_unit(b, blk)
-                if blk == 0:
-                    prepare_forward(b)
-                if blk * BLOCK == HALF:
-                    prepare_backward(b)
-                if b == 0:
-                    prepare_weight_block(wf_raw, wf_q, blk)
-                out_unit(b, blk)
+        def operand_of_round(b, blk):
+            if blk + AHEAD < N_BLOCKS:
+                raw, w_q = (wg_raw, wg_q) if b == 0 else (wf_raw, wf_q)
+                return raw[blk + AHEAD][:], IN_ORDER, columns(w_q, block_cols(blk + AHEAD))
+            if blk * BLOCK == HALF:
+                return adj_sb[b][:], BY_RESIDUE, columns(bwd_q[b], slice(0, NODES))
+            return None
+
+        ident = keep.tile([P, P], F32, name="ident")
+        masks.make_identity(nc, ident[:])
+        eps_col = keep.tile([P, 1], F32, name="eps_col")
+        nc.vector.memset(eps_col[:], EPS)
+        params_f32 = keep.tile([P, P], F32, name="params_f32")
+        nc.vector.memset(params_f32[:], 0.0)
+        ln_cols = keep.tile([P, 2 * PACK], F32, name="ln_cols")
+
+        wg_grouped = interleave_weight_block(nc.scalar.copy, wg_raw, 0)
+        wf_grouped = interleave_weight_block(nc.scalar.copy, wf_raw, 0)
+        statistics(0)
+        nc.vector.tensor_copy(out=params_f32[0 : 2 * PACK, :], in_=params_rows[:])
+        params_t = psum.tile([P, P], F32, tag="bank", name="params_t")
+        nc.tensor.transpose(params_t[:], params_f32[:], ident[:])
+        statistics(1)
+        nc.scalar.activation(out=std[:], in_=mean_var[:, :, 1], func=ACT.Sqrt, bias=eps_col[:])
+        nc.vector.tensor_copy(out=ln_cols[:], in_=params_t[:, 0 : 2 * PACK])
+        quantise(nc, columns(wg_q, block_cols(0)), wg_grouped[:])
+        quantise(nc, columns(wf_q, block_cols(0)), wf_grouped[:])
+        nc.vector.reciprocal(out=rstd[:], in_=std[:])
+        normalise(0)
+        normalise(1)
+        wg_grouped = interleave_weight_block(nc.scalar.copy, wg_raw, 1)
+        transpose_xn(0)
+        xn_grouped0 = interleave_xn(0)
+        transpose_xn(1)
+        quantise(nc, columns(xn_q[0], slice(0, NODES)), xn_grouped0[:])
+        xn_grouped1 = interleave_xn(1)
+        wf_grouped = interleave_weight_block(nc.scalar.copy, wf_raw, 1)
+        fwd_grouped = [transpose_adjacency(b) for b in range(GRAPHS)]
+        quantise(nc, columns(wg_q, block_cols(1)), wg_grouped[:])
+        quantise(nc, columns(xn_q[1], slice(0, NODES)), xn_grouped1[:])
+        quantise(nc, columns(wf_q, block_cols(1)), wf_grouped[:])
+        for b in range(GRAPHS):
+            quantise(nc, columns(fwd_q[b], slice(0, NODES)), fwd_grouped[b][:])
+
+        units = [(b, blk) for blk in range(N_BLOCKS) for b in range(GRAPHS)]
+        for i in range(len(units) + 1):
+            if i < len(units):
+                b, blk = units[i]
+                g_grouped = g_matmuls(b, blk)
+                operand = operand_of_round(b, blk)
+                if operand is not None:
+                    rows, order, target = operand
+                    grouped = stage.tile([P, BLOCK, PACK], BF16, name="late_grouped", bufs=2, align_bytes=64)
+                    interleave_rows(nc.vector.tensor_copy, grouped[:], order, rows)
+                quantise(nc, columns(g_q[b], block_cols(blk)), g_grouped[:])
+                if operand is not None:
+                    quantise(nc, target, grouped[:])
+            if i > 0:
+                b, blk = units[i - 1]
+                out_matmuls(b, blk)

@@ -45,7 +45,6 @@ def quantise(nc, operand, grouped):
 def tile_encoderblock_pb_kernel(tc, x_attn, adj, ln2_g, ln2_b, w_fc1, w_gcn, out):
     nc = tc.nc
     with ExitStack() as ctx:
-        ctx.enter_context(tc.manual_schedule())
         keep = ctx.enter_context(tc.tile_pool(name="keep", bufs=1))
         stage = ctx.enter_context(tc.tile_pool(name="stage", bufs=3))
         results = ctx.enter_context(tc.tile_pool(name="results", bufs=8))

@@ -70,6 +70,16 @@ def tile_encoderblock_pb_kernel(tc, x_attn, adj, ln2_g, ln2_b, w_fc1, w_gcn, out
         wg_q = mx_operand("wg", HIDDEN)
         wf_q = mx_operand("wf", HIDDEN)
 
+        eps_col = keep.tile([P, 1], F32, name="eps_col")
+        nc.gpsimd.memset(eps_col[:], EPS)
+        table_col = keep.tile([P, 1], F32, name="table_col")
+        nc.scalar.activation(out=table_col[:], in_=eps_col[:], func=ACT.Abs_reciprocal_sqrt)
+        ident = keep.tile([P, P], F32, name="ident")
+        masks.make_identity(nc, ident[:])
+        params_f32 = keep.tile([P, P], F32, name="params_f32")
+        nc.gpsimd.memset(params_f32[:], 0.0)
+        ln_cols = keep.tile([P, 2 * PACK], F32, name="ln_cols")
+
         params_rows = keep.tile([2 * PACK, P], BF16, name="params_rows")
         nc.scalar.dma_start(out=params_rows[0:PACK, :], in_=ln2_g.rearrange("(u c) -> u c", c=P))
         nc.scalar.dma_start(out=params_rows[PACK : 2 * PACK, :], in_=ln2_b.rearrange("(u c) -> u c", c=P))
@@ -99,7 +109,6 @@ def tile_encoderblock_pb_kernel(tc, x_attn, adj, ln2_g, ln2_b, w_fc1, w_gcn, out
 
         stats = keep.tile([P, GRAPHS * PACK, 6], F32, name="stats")
         mean_var = keep.tile([P, GRAPHS * PACK, 2], F32, name="mean_var")
-        std = keep.tile([P, GRAPHS * PACK], F32, name="std")
         rstd = keep.tile([P, GRAPHS * PACK], F32, name="rstd")
         xhat = [keep.tile([P, PACK, FEATS], F32, name="xhat%d" % b) for b in range(GRAPHS)]
         planes = [keep.tile([P, PACK, NODES], BF16, name="planes%d" % b) for b in range(GRAPHS)]
@@ -204,26 +213,17 @@ def tile_encoderblock_pb_kernel(tc, x_attn, adj, ln2_g, ln2_b, w_fc1, w_gcn, out
                 return adj_sb[b][:], BY_RESIDUE, columns(bwd_q[b], slice(0, NODES))
             return None
 
-        ident = keep.tile([P, P], F32, name="ident")
-        masks.make_identity(nc, ident[:])
-        eps_col = keep.tile([P, 1], F32, name="eps_col")
-        nc.vector.memset(eps_col[:], EPS)
-        params_f32 = keep.tile([P, P], F32, name="params_f32")
-        nc.vector.memset(params_f32[:], 0.0)
-        ln_cols = keep.tile([P, 2 * PACK], F32, name="ln_cols")
-
         wg_grouped = interleave_weight_block(nc.scalar.copy, wg_raw, 0)
         wf_grouped = interleave_weight_block(nc.scalar.copy, wf_raw, 0)
         statistics(0)
-        nc.vector.tensor_copy(out=params_f32[0 : 2 * PACK, :], in_=params_rows[:])
+        nc.gpsimd.tensor_copy(out=params_f32[0 : 2 * PACK, :], in_=params_rows[:])
         params_t = psum.tile([P, P], F32, tag="bank", name="params_t")
         nc.tensor.transpose(params_t[:], params_f32[:], ident[:])
         statistics(1)
-        nc.scalar.activation(out=std[:], in_=mean_var[:, :, 1], func=ACT.Sqrt, bias=eps_col[:])
-        nc.vector.tensor_copy(out=ln_cols[:], in_=params_t[:, 0 : 2 * PACK])
+        nc.scalar.activation(out=rstd[:], in_=mean_var[:, :, 1], func=ACT.Abs_reciprocal_sqrt, bias=eps_col[:])
+        nc.scalar.copy(out=ln_cols[:], in_=params_t[:, 0 : 2 * PACK])
         quantise(nc, columns(wg_q, block_cols(0)), wg_grouped[:])
         quantise(nc, columns(wf_q, block_cols(0)), wf_grouped[:])
-        nc.vector.reciprocal(out=rstd[:], in_=std[:])
         normalise(0)
         normalise(1)
         wg_grouped = interleave_weight_block(nc.scalar.copy, wg_raw, 1)

@@ -50,7 +50,9 @@ def tile_encoderblock_pb_kernel(tc, x_attn, adj, ln2_g, ln2_b, w_fc1, w_gcn, out
         results = ctx.enter_context(tc.tile_pool(name="results", bufs=8))
         psum = ctx.enter_context(tc.psum_pool(name="psum", bufs=8))
 
-        x_sb = [keep.tile([P, PACK, FEATS], BF16, name="x_sb%d" % b) for b in range(GRAPHS)]
+        x_sb = [
+            [keep.tile([P, PACK // 2, FEATS], BF16, name="x_sb%d%d" % (b, h)) for h in range(2)] for b in range(GRAPHS)
+        ]
         adj_sb = [keep.tile([P, PACK, NODES], BF16, name="adj_sb%d" % b) for b in range(GRAPHS)]
         wg_raw = [keep.tile([P, PACK, BLOCK], BF16, name="wg_raw%d" % blk) for blk in range(N_BLOCKS)]
         wf_raw = [keep.tile([P, PACK, BLOCK], BF16, name="wf_raw%d" % blk) for blk in range(N_BLOCKS)]
@@ -84,20 +86,25 @@ def tile_encoderblock_pb_kernel(tc, x_attn, adj, ln2_g, ln2_b, w_fc1, w_gcn, out
         nc.scalar.dma_start(out=params_rows[0:PACK, :], in_=ln2_g.rearrange("(u c) -> u c", c=P))
         nc.scalar.dma_start(out=params_rows[PACK : 2 * PACK, :], in_=ln2_b.rearrange("(u c) -> u c", c=P))
 
-        def load_nodes(dst, src):
+        def load_adjacency(dst, src):
             nc.sync.dma_start(out=dst[:], in_=src.rearrange("(p t) c -> p t c", t=PACK))
+
+        def load_x(b):
+            rows = x_attn[b].rearrange("(p t) c -> p t c", t=PACK)
+            for h in range(2):
+                nc.sync.dma_start(out=x_sb[b][h][:], in_=rows[:, 2 * h : 2 * h + 2, :])
 
         def load_weight_block(dst, src, blk):
             nc.sync.dma_start(out=dst[blk][:], in_=src.rearrange("(u p) n -> p u n", p=P)[:, :, block_cols(blk)])
 
-        load_nodes(x_sb[0], x_attn[0])
+        load_x(0)
         load_weight_block(wg_raw, w_gcn, 0)
-        load_nodes(x_sb[1], x_attn[1])
+        load_x(1)
         load_weight_block(wf_raw, w_fc1, 0)
         load_weight_block(wg_raw, w_gcn, 1)
         load_weight_block(wf_raw, w_fc1, 1)
-        load_nodes(adj_sb[0], adj[0])
-        load_nodes(adj_sb[1], adj[1])
+        load_adjacency(adj_sb[0], adj[0])
+        load_adjacency(adj_sb[1], adj[1])
         for blk in range(AHEAD, N_BLOCKS):
             load_weight_block(wg_raw, w_gcn, blk)
             load_weight_block(wf_raw, w_fc1, blk)
@@ -108,24 +115,27 @@ def tile_encoderblock_pb_kernel(tc, x_attn, adj, ln2_g, ln2_b, w_fc1, w_gcn, out
             return grouped
 
         stats = keep.tile([P, GRAPHS * PACK, 6], F32, name="stats")
-        mean_var = keep.tile([P, GRAPHS * PACK, 2], F32, name="mean_var")
-        rstd = keep.tile([P, GRAPHS * PACK], F32, name="rstd")
+        mean_var = [keep.tile([P, PACK, 2], F32, name="mean_var%d" % b) for b in range(GRAPHS)]
+        rstd = [keep.tile([P, PACK], F32, name="rstd%d" % b) for b in range(GRAPHS)]
         xhat = [keep.tile([P, PACK, FEATS], F32, name="xhat%d" % b) for b in range(GRAPHS)]
         planes = [keep.tile([P, PACK, NODES], BF16, name="planes%d" % b) for b in range(GRAPHS)]
 
         def statistics(b):
             for t in range(PACK):
-                nc.vector.bn_stats(out=stats[:, b * PACK + t, :], in_=x_sb[b][:, t, :])
+                nc.vector.bn_stats(out=stats[:, b * PACK + t, :], in_=x_sb[b][t // 2][:, t % 2, :])
             for t in range(PACK):
-                nc.vector.bn_aggr(out=mean_var[:, b * PACK + t, :], in_=stats[:, b * PACK + t, :])
+                nc.vector.bn_aggr(out=mean_var[b][:, t, :], in_=stats[:, b * PACK + t, :])
+            nc.scalar.activation(
+                out=rstd[b][:], in_=mean_var[b][:, :, 1], func=ACT.Abs_reciprocal_sqrt, bias=eps_col[:]
+            )
 
         def normalise(b):
             for t in range(PACK):
                 nc.vector.tensor_scalar(
                     out=xhat[b][:, t, :],
-                    in0=x_sb[b][:, t, :],
-                    scalar1=mean_var[:, b * PACK + t, 0:1],
-                    scalar2=rstd[:, b * PACK + t : b * PACK + t + 1],
+                    in0=x_sb[b][t // 2][:, t % 2, :],
+                    scalar1=mean_var[b][:, t, 0:1],
+                    scalar2=rstd[b][:, t : t + 1],
                     op0=ALU.subtract,
                     op1=ALU.mult,
                 )
@@ -138,12 +148,7 @@ def tile_encoderblock_pb_kernel(tc, x_attn, adj, ln2_g, ln2_b, w_fc1, w_gcn, out
                 flat = bank[:].rearrange("p t n -> p (t n)")
                 gain = ln_cols[:, u : u + 1]
                 shift = ln_cols[:, PACK + u : PACK + u + 1]
-                if u % 2 == 0:
-                    nc.scalar.activation(out=planes[b][:, u, :], in_=flat, func=ACT.Identity, scale=gain, bias=shift)
-                else:
-                    nc.vector.tensor_scalar(
-                        out=planes[b][:, u, :], in0=flat, scalar1=gain, scalar2=shift, op0=ALU.mult, op1=ALU.add
-                    )
+                nc.scalar.activation(out=planes[b][:, u, :], in_=flat, func=ACT.Identity, scale=gain, bias=shift)
 
         def interleave_xn(b):
             grouped = stage.tile([P, NODES, PACK], BF16, name="xn_grouped", bufs=2, align_bytes=64)
@@ -180,14 +185,15 @@ def tile_encoderblock_pb_kernel(tc, x_attn, adj, ln2_g, ln2_b, w_fc1, w_gcn, out
                 stop=stop,
             )
 
-        def g_matmuls(b, blk):
+        def g_matmuls(b, blk, shared):
             grouped = stage.tile([P, BLOCK, PACK], BF16, name="g_grouped", align_bytes=64)
             for q in range(BLOCK // P):
                 bank = psum.tile([P, PACK, P], F32, tag="bank", name="g_bank")
                 cols = slice(blk * BLOCK + q * P, blk * BLOCK + (q + 1) * P)
                 for t in range(PACK):
                     mx_pass(bank[:, t, :], xn_q[b], t, wg_q, cols, True, True)
-                nc.scalar.copy(out=grouped[:, q * P : (q + 1) * P, :], in_=bank[:].rearrange("p t w -> p w t"))
+                copy = nc.vector.tensor_copy if shared and q % 2 else nc.scalar.copy
+                copy(out=grouped[:, q * P : (q + 1) * P, :], in_=bank[:].rearrange("p t w -> p w t"))
             return grouped
 
         def out_matmuls(b, blk):
@@ -220,7 +226,6 @@ def tile_encoderblock_pb_kernel(tc, x_attn, adj, ln2_g, ln2_b, w_fc1, w_gcn, out
         params_t = psum.tile([P, P], F32, tag="bank", name="params_t")
         nc.tensor.transpose(params_t[:], params_f32[:], ident[:])
         statistics(1)
-        nc.scalar.activation(out=rstd[:], in_=mean_var[:, :, 1], func=ACT.Abs_reciprocal_sqrt, bias=eps_col[:])
         nc.scalar.copy(out=ln_cols[:], in_=params_t[:, 0 : 2 * PACK])
         quantise(nc, columns(wg_q, block_cols(0)), wg_grouped[:])
         quantise(nc, columns(wf_q, block_cols(0)), wf_grouped[:])
@@ -232,7 +237,7 @@ def tile_encoderblock_pb_kernel(tc, x_attn, adj, ln2_g, ln2_b, w_fc1, w_gcn, out
         transpose_xn(1)
         quantise(nc, columns(xn_q[0], slice(0, NODES)), xn_grouped0[:])
         xn_grouped1 = interleave_xn(1)
-        wf_grouped = interleave_weight_block(nc.scalar.copy, wf_raw, 1)
+        wf_grouped = interleave_weight_block(nc.vector.tensor_copy, wf_raw, 1)
         fwd_grouped = [transpose_adjacency(b) for b in range(GRAPHS)]
         quantise(nc, columns(wg_q, block_cols(1)), wg_grouped[:])
         quantise(nc, columns(xn_q[1], slice(0, NODES)), xn_grouped1[:])
@@ -244,7 +249,7 @@ def tile_encoderblock_pb_kernel(tc, x_attn, adj, ln2_g, ln2_b, w_fc1, w_gcn, out
         for i in range(len(units) + 1):
             if i < len(units):
                 b, blk = units[i]
-                g_grouped = g_matmuls(b, blk)
+                g_grouped = g_matmuls(b, blk, i >= len(units) - 2)
                 operand = operand_of_round(b, blk)
                 if operand is not None:
                     rows, order, target = operand

@@ -50,9 +50,7 @@ def tile_encoderblock_pb_kernel(tc, x_attn, adj, ln2_g, ln2_b, w_fc1, w_gcn, out
         results = ctx.enter_context(tc.tile_pool(name="results", bufs=8))
         psum = ctx.enter_context(tc.psum_pool(name="psum", bufs=8))
 
-        x_sb = [
-            [keep.tile([P, PACK // 2, FEATS], BF16, name="x_sb%d%d" % (b, h)) for h in range(2)] for b in range(GRAPHS)
-        ]
+        x_sb = [keep.tile([P, PACK, FEATS], BF16, name="x_sb%d" % b) for b in range(GRAPHS)]
         adj_sb = [keep.tile([P, PACK, NODES], BF16, name="adj_sb%d" % b) for b in range(GRAPHS)]
         wg_raw = [keep.tile([P, PACK, BLOCK], BF16, name="wg_raw%d" % blk) for blk in range(N_BLOCKS)]
         wf_raw = [keep.tile([P, PACK, BLOCK], BF16, name="wf_raw%d" % blk) for blk in range(N_BLOCKS)]
@@ -86,25 +84,20 @@ def tile_encoderblock_pb_kernel(tc, x_attn, adj, ln2_g, ln2_b, w_fc1, w_gcn, out
         nc.scalar.dma_start(out=params_rows[0:PACK, :], in_=ln2_g.rearrange("(u c) -> u c", c=P))
         nc.scalar.dma_start(out=params_rows[PACK : 2 * PACK, :], in_=ln2_b.rearrange("(u c) -> u c", c=P))
 
-        def load_adjacency(dst, src):
+        def load_nodes(dst, src):
             nc.sync.dma_start(out=dst[:], in_=src.rearrange("(p t) c -> p t c", t=PACK))
-
-        def load_x(b):
-            rows = x_attn[b].rearrange("(p t) c -> p t c", t=PACK)
-            for h in range(2):
-                nc.sync.dma_start(out=x_sb[b][h][:], in_=rows[:, 2 * h : 2 * h + 2, :])
 
         def load_weight_block(dst, src, blk):
             nc.sync.dma_start(out=dst[blk][:], in_=src.rearrange("(u p) n -> p u n", p=P)[:, :, block_cols(blk)])
 
-        load_x(0)
+        load_nodes(x_sb[0], x_attn[0])
         load_weight_block(wg_raw, w_gcn, 0)
-        load_x(1)
+        load_nodes(x_sb[1], x_attn[1])
         load_weight_block(wf_raw, w_fc1, 0)
         load_weight_block(wg_raw, w_gcn, 1)
         load_weight_block(wf_raw, w_fc1, 1)
-        load_adjacency(adj_sb[0], adj[0])
-        load_adjacency(adj_sb[1], adj[1])
+        load_nodes(adj_sb[0], adj[0])
+        load_nodes(adj_sb[1], adj[1])
         for blk in range(AHEAD, N_BLOCKS):
             load_weight_block(wg_raw, w_gcn, blk)
             load_weight_block(wf_raw, w_fc1, blk)
@@ -122,7 +115,7 @@ def tile_encoderblock_pb_kernel(tc, x_attn, adj, ln2_g, ln2_b, w_fc1, w_gcn, out
 
         def statistics(b):
             for t in range(PACK):
-                nc.vector.bn_stats(out=stats[:, b * PACK + t, :], in_=x_sb[b][t // 2][:, t % 2, :])
+                nc.vector.bn_stats(out=stats[:, b * PACK + t, :], in_=x_sb[b][:, t, :])
             for t in range(PACK):
                 nc.vector.bn_aggr(out=mean_var[b][:, t, :], in_=stats[:, b * PACK + t, :])
             nc.scalar.activation(
@@ -133,7 +126,7 @@ def tile_encoderblock_pb_kernel(tc, x_attn, adj, ln2_g, ln2_b, w_fc1, w_gcn, out
             for t in range(PACK):
                 nc.vector.tensor_scalar(
                     out=xhat[b][:, t, :],
-                    in0=x_sb[b][t // 2][:, t % 2, :],
+                    in0=x_sb[b][:, t, :],
                     scalar1=mean_var[b][:, t, 0:1],
                     scalar2=rstd[b][:, t : t + 1],
                     op0=ALU.subtract,
@@ -185,15 +178,14 @@ def tile_encoderblock_pb_kernel(tc, x_attn, adj, ln2_g, ln2_b, w_fc1, w_gcn, out
                 stop=stop,
             )
 
-        def g_matmuls(b, blk, shared):
+        def g_matmuls(b, blk):
             grouped = stage.tile([P, BLOCK, PACK], BF16, name="g_grouped", align_bytes=64)
             for q in range(BLOCK // P):
                 bank = psum.tile([P, PACK, P], F32, tag="bank", name="g_bank")
                 cols = slice(blk * BLOCK + q * P, blk * BLOCK + (q + 1) * P)
                 for t in range(PACK):
                     mx_pass(bank[:, t, :], xn_q[b], t, wg_q, cols, True, True)
-                copy = nc.vector.tensor_copy if shared and q % 2 else nc.scalar.copy
-                copy(out=grouped[:, q * P : (q + 1) * P, :], in_=bank[:].rearrange("p t w -> p w t"))
+                nc.scalar.copy(out=grouped[:, q * P : (q + 1) * P, :], in_=bank[:].rearrange("p t w -> p w t"))
             return grouped
 
         def out_matmuls(b, blk):
@@ -249,7 +241,7 @@ def tile_encoderblock_pb_kernel(tc, x_attn, adj, ln2_g, ln2_b, w_fc1, w_gcn, out
         for i in range(len(units) + 1):
             if i < len(units):
                 b, blk = units[i]
-                g_grouped = g_matmuls(b, blk, i >= len(units) - 2)
+                g_grouped = g_matmuls(b, blk)
                 operand = operand_of_round(b, blk)
                 if operand is not None:
                     rows, order, target = operand

from contextlib import ExitStack

import concourse.masks as masks
import concourse.mybir as mybir

F32 = mybir.dt.float32
BF16 = mybir.dt.bfloat16
U32 = mybir.dt.uint32
U8 = mybir.dt.uint8
FP8X4 = mybir.dt.float8_e4m3fn_x4
ACT = mybir.ActivationFunctionType
ALU = mybir.AluOpType

P = 128
PACK = 4
GRAPHS = 2
NODES = 512
FEATS = 512
HIDDEN = 2048
HALF = HIDDEN // 2
BLOCK = 512
N_BLOCKS = HIDDEN // BLOCK
AHEAD = 2
EPS = 1e-5

FLOPS = 2 * GRAPHS * NODES * FEATS * 2 * HIDDEN + 2 * GRAPHS * NODES * NODES * HIDDEN

IN_ORDER = "p (c i) t -> p c t i"
BY_RESIDUE = "p (i c) t -> p c t i"


def block_cols(blk):
    return slice(blk * BLOCK, (blk + 1) * BLOCK)


def interleave_rows(copy, grouped, order, rows):
    copy(out=grouped.rearrange(order, i=PACK), in_=rows.rearrange("p t (c i) -> p c t i", i=PACK))


def quantise(nc, operand, grouped):
    codes, scales = operand
    nc.vector.quantize_mx(out=codes.bitcast(FP8X4), scales=scales, in_=grouped.rearrange("p n t -> p (n t)"))


def tile_encoderblock_pb_kernel(tc, x_attn, adj, ln2_g, ln2_b, w_fc1, w_gcn, out):
    nc = tc.nc
    with ExitStack() as ctx:
        keep = ctx.enter_context(tc.tile_pool(name="keep", bufs=1))
        stage = ctx.enter_context(tc.tile_pool(name="stage", bufs=3))
        results = ctx.enter_context(tc.tile_pool(name="results", bufs=8))
        psum = ctx.enter_context(tc.psum_pool(name="psum", bufs=8))

        x_sb = [keep.tile([P, PACK, FEATS], BF16, name="x_sb%d" % b) for b in range(GRAPHS)]
        adj_sb = [keep.tile([P, PACK, NODES], BF16, name="adj_sb%d" % b) for b in range(GRAPHS)]
        wg_raw = [keep.tile([P, PACK, BLOCK], BF16, name="wg_raw%d" % blk) for blk in range(N_BLOCKS)]
        wf_raw = [keep.tile([P, PACK, BLOCK], BF16, name="wf_raw%d" % blk) for blk in range(N_BLOCKS)]

        def mx_operand(name, width):
            codes = keep.tile([P, width], U32, name=name + "_codes", align_bytes=64)
            scales = keep.tile([P, width], U8, name=name + "_scales", align_bytes=64)
            return codes, scales

        def columns(operand, cols):
            return operand[0][:, cols], operand[1][:, cols]

        xn_q = [mx_operand("xn%d" % b, NODES) for b in range(GRAPHS)]
        fwd_q = [mx_operand("fwd%d" % b, NODES) for b in range(GRAPHS)]
        bwd_q = [mx_operand("bwd%d" % b, NODES) for b in range(GRAPHS)]
        g_q = [mx_operand("g%d" % b, HIDDEN) for b in range(GRAPHS)]
        wg_q = mx_operand("wg", HIDDEN)
        wf_q = mx_operand("wf", HIDDEN)

        eps_col = keep.tile([P, 1], F32, name="eps_col")
        nc.gpsimd.memset(eps_col[:], EPS)
        table_col = keep.tile([P, 1], F32, name="table_col")
        nc.scalar.activation(out=table_col[:], in_=eps_col[:], func=ACT.Abs_reciprocal_sqrt)
        ident = keep.tile([P, P], F32, name="ident")
        masks.make_identity(nc, ident[:])
        params_f32 = keep.tile([P, P], F32, name="params_f32")
        nc.gpsimd.memset(params_f32[:], 0.0)
        ln_cols = keep.tile([P, 2 * PACK], F32, name="ln_cols")

        params_rows = keep.tile([2 * PACK, P], BF16, name="params_rows")
        nc.scalar.dma_start(out=params_rows[0:PACK, :], in_=ln2_g.rearrange("(u c) -> u c", c=P))
        nc.scalar.dma_start(out=params_rows[PACK : 2 * PACK, :], in_=ln2_b.rearrange("(u c) -> u c", c=P))

        def load_nodes(dst, src):
            nc.sync.dma_start(out=dst[:], in_=src.rearrange("(p t) c -> p t c", t=PACK))

        def load_weight_block(dst, src, blk):
            nc.sync.dma_start(out=dst[blk][:], in_=src.rearrange("(u p) n -> p u n", p=P)[:, :, block_cols(blk)])

        load_nodes(x_sb[0], x_attn[0])
        load_weight_block(wg_raw, w_gcn, 0)
        load_nodes(x_sb[1], x_attn[1])
        load_weight_block(wf_raw, w_fc1, 0)
        load_weight_block(wg_raw, w_gcn, 1)
        load_weight_block(wf_raw, w_fc1, 1)
        load_nodes(adj_sb[0], adj[0])
        load_nodes(adj_sb[1], adj[1])
        for blk in range(AHEAD, N_BLOCKS):
            load_weight_block(wg_raw, w_gcn, blk)
            load_weight_block(wf_raw, w_fc1, blk)

        def interleave_weight_block(copy, raw, blk):
            grouped = stage.tile([P, BLOCK, PACK], BF16, name="w_grouped", bufs=4, align_bytes=64)
            interleave_rows(copy, grouped[:], IN_ORDER, raw[blk][:])
            return grouped

        stats = keep.tile([P, GRAPHS * PACK, 6], F32, name="stats")
        mean_var = [keep.tile([P, PACK, 2], F32, name="mean_var%d" % b) for b in range(GRAPHS)]
        rstd = [keep.tile([P, PACK], F32, name="rstd%d" % b) for b in range(GRAPHS)]
        xhat = [keep.tile([P, PACK, FEATS], F32, name="xhat%d" % b) for b in range(GRAPHS)]
        planes = [keep.tile([P, PACK, NODES], BF16, name="planes%d" % b) for b in range(GRAPHS)]

        def statistics(b):
            for t in range(PACK):
                nc.vector.bn_stats(out=stats[:, b * PACK + t, :], in_=x_sb[b][:, t, :])
            for t in range(PACK):
                nc.vector.bn_aggr(out=mean_var[b][:, t, :], in_=stats[:, b * PACK + t, :])
            nc.scalar.activation(
                out=rstd[b][:], in_=mean_var[b][:, :, 1], func=ACT.Abs_reciprocal_sqrt, bias=eps_col[:]
            )

        def normalise(b):
            for t in range(PACK):
                nc.vector.tensor_scalar(
                    out=xhat[b][:, t, :],
                    in0=x_sb[b][:, t, :],
                    scalar1=mean_var[b][:, t, 0:1],
                    scalar2=rstd[b][:, t : t + 1],
                    op0=ALU.subtract,
                    op1=ALU.mult,
                )

        def transpose_xn(b):
            for u in range(PACK):
                bank = psum.tile([P, PACK, P], F32, tag="bank", name="xt_bank")
                for t in range(PACK):
                    nc.tensor.transpose(bank[:, t, :], xhat[b][:, t, u * P : (u + 1) * P], ident[:])
                flat = bank[:].rearrange("p t n -> p (t n)")
                gain = ln_cols[:, u : u + 1]
                shift = ln_cols[:, PACK + u : PACK + u + 1]
                nc.scalar.activation(out=planes[b][:, u, :], in_=flat, func=ACT.Identity, scale=gain, bias=shift)

        def interleave_xn(b):
            grouped = stage.tile([P, NODES, PACK], BF16, name="xn_grouped", bufs=2, align_bytes=64)
            interleave_rows(nc.vector.tensor_copy, grouped[:], IN_ORDER, planes[b][:])
            return grouped

        def transpose_adjacency(b):
            words = adj_sb[b][:].rearrange("p s j -> p (s j)").bitcast(F32)
            words = words.rearrange("p (s q v) -> p s v q", s=PACK, v=2)
            grouped = stage.tile([P, NODES, PACK], BF16, name="fwd_grouped", bufs=2, align_bytes=64)
            grouped_words = grouped[:].rearrange("p n t -> p (n t)").bitcast(F32)
            grouped_words = grouped_words.rearrange("p (s m v) -> p s m v", s=PACK, v=2)
            for pair in range(PACK // 2):
                bank = psum.tile([P, 2, 2, P], F32, tag="bank", name="adjt_bank")
                for s2 in range(2):
                    for v in range(2):
                        nc.tensor.transpose(bank[:, s2, v, :], words[:, 2 * pair + s2, v, :], ident[:])
                nc.scalar.copy(
                    out=grouped_words[:, 2 * pair : 2 * pair + 2, :, :],
                    in_=bank[:].rearrange("p s v m -> p s m v"),
                )
            return grouped

        def mx_pass(acc, stationary, s, moving, cols, start, stop):
            lhs_codes, lhs_scales = columns(stationary, slice(s * P, (s + 1) * P))
            rhs_codes, rhs_scales = columns(moving, cols)
            nc.tensor.matmul_mx(
                out=acc,
                lhsT=lhs_codes.bitcast(FP8X4),
                lhsT_scale=lhs_scales,
                rhs=rhs_codes.bitcast(FP8X4),
                rhs_scale=rhs_scales,
                start=start,
                stop=stop,
            )

        def g_matmuls(b, blk):
            grouped = stage.tile([P, BLOCK, PACK], BF16, name="g_grouped", align_bytes=64)
            for q in range(BLOCK // P):
                bank = psum.tile([P, PACK, P], F32, tag="bank", name="g_bank")
                cols = slice(blk * BLOCK + q * P, blk * BLOCK + (q + 1) * P)
                for t in range(PACK):
                    mx_pass(bank[:, t, :], xn_q[b], t, wg_q, cols, True, True)
                nc.scalar.copy(out=grouped[:, q * P : (q + 1) * P, :], in_=bank[:].rearrange("p t w -> p w t"))
            return grouped

        def out_matmuls(b, blk):
            cols = block_cols(blk)
            adj_q = fwd_q[b] if blk * BLOCK < HALF else bwd_q[b]
            out_rows = out[b].rearrange("(m s) f -> m s f", s=PACK)
            for s in range(PACK):
                acc = psum.tile([P, BLOCK], F32, tag="bank", name="acc")
                mx_pass(acc[:], xn_q[b], s, wf_q, cols, True, False)
                mx_pass(acc[:], adj_q, s, g_q[b], cols, False, True)
                res = results.tile([P, BLOCK], F32, name="res")
                if s % 2 == 0:
                    nc.scalar.activation(out=res[:], in_=acc[:], func=ACT.Relu)
                else:
                    nc.vector.tensor_scalar_max(out=res[:], in0=acc[:], scalar1=0.0)
                nc.sync.dma_start(out=out_rows[:, s, cols], in_=res[:])

        def operand_of_round(b, blk):
            if blk + AHEAD < N_BLOCKS:
                raw, w_q = (wg_raw, wg_q) if b == 0 else (wf_raw, wf_q)
                return raw[blk + AHEAD][:], IN_ORDER, columns(w_q, block_cols(blk + AHEAD))
            if blk * BLOCK == HALF:
                return adj_sb[b][:], BY_RESIDUE, columns(bwd_q[b], slice(0, NODES))
            return None

        wg_grouped = interleave_weight_block(nc.scalar.copy, wg_raw, 0)
        wf_grouped = interleave_weight_block(nc.scalar.copy, wf_raw, 0)
        statistics(0)
        nc.gpsimd.tensor_copy(out=params_f32[0 : 2 * PACK, :], in_=params_rows[:])
        params_t = psum.tile([P, P], F32, tag="bank", name="params_t")
        nc.tensor.transpose(params_t[:], params_f32[:], ident[:])
        statistics(1)
        nc.scalar.copy(out=ln_cols[:], in_=params_t[:, 0 : 2 * PACK])
        quantise(nc, columns(wg_q, block_cols(0)), wg_grouped[:])
        quantise(nc, columns(wf_q, block_cols(0)), wf_grouped[:])
        normalise(0)
        normalise(1)
        wg_grouped = interleave_weight_block(nc.scalar.copy, wg_raw, 1)
        transpose_xn(0)
        xn_grouped0 = interleave_xn(0)
        transpose_xn(1)
        quantise(nc, columns(xn_q[0], slice(0, NODES)), xn_grouped0[:])
        xn_grouped1 = interleave_xn(1)
        wf_grouped = interleave_weight_block(nc.vector.tensor_copy, wf_raw, 1)
        fwd_grouped = [transpose_adjacency(b) for b in range(GRAPHS)]
        quantise(nc, columns(wg_q, block_cols(1)), wg_grouped[:])
        quantise(nc, columns(xn_q[1], slice(0, NODES)), xn_grouped1[:])
        quantise(nc, columns(wf_q, block_cols(1)), wf_grouped[:])
        for b in range(GRAPHS):
            quantise(nc, columns(fwd_q[b], slice(0, NODES)), fwd_grouped[b][:])

        units = [(b, blk) for blk in range(N_BLOCKS) for b in range(GRAPHS)]
        for i in range(len(units) + 1):
            if i < len(units):
                b, blk = units[i]
                g_grouped = g_matmuls(b, blk)
                operand = operand_of_round(b, blk)
                if operand is not None:
                    rows, order, target = operand
                    grouped = stage.tile([P, BLOCK, PACK], BF16, name="late_grouped", bufs=2, align_bytes=64)
                    interleave_rows(nc.vector.tensor_copy, grouped[:], order, rows)
                quantise(nc, columns(g_q[b], block_cols(blk)), g_grouped[:])
                if operand is not None:
                    quantise(nc, target, grouped[:])
            if i > 0:
                b, blk = units[i - 1]
                out_matmuls(b, blk)
